import numpy as np
import ml_dtypes


def mxq(x, axis, fmt="e4m3"):
    dtype, down = {"e4m3": (ml_dtypes.float8_e4m3fn, 7), "e5m2": (ml_dtypes.float8_e5m2, 14)}[fmt]
    v = np.moveaxis(np.asarray(x, np.float32).astype(ml_dtypes.bfloat16).astype(np.float64), axis, -1)
    blocks = v.reshape(v.shape[:-1] + (-1, 32))
    amax = np.abs(blocks).max(-1, keepdims=True)
    byte = np.maximum(np.where(amax > 0, np.frexp(amax)[1] - 1 + 127, 0) - down, 1)
    scale = np.exp2(byte - 127.0)
    codes = (blocks / scale).astype(np.float32).astype(dtype).astype(np.float64)
    return np.moveaxis((codes * scale).reshape(v.shape), -1, axis)


WIDE = False


def mx_kscale(k):
    if not WIDE:
        return np.ones(k)
    levels = np.array([10, -10, 5, -5, 0])
    a = np.random.permutation(np.resize(levels, k // 512 * 4)).reshape(k // 512, 4)
    idx = np.arange(k)
    return np.exp2(a[idx // 512, idx % 128 // 32])


BF16 = ml_dtypes.bfloat16


def bf(x):
    return np.asarray(x, np.float32).astype(BF16)


def f64(x):
    return np.asarray(x).astype(np.float64)


E2M1 = np.array([0.0, 0.5, 1.0, 1.5, 2.0, 3.0, 4.0, 6.0, -0.0, -0.5, -1.0, -1.5, -2.0, -3.0, -4.0, -6.0])


def pack_weight(w, fmt):
    k, n = w.shape
    w = f64(bf(w)).reshape(k // 32, 32, n)
    amax = np.abs(w).max(1)
    if fmt == "e4m3":
        byte = np.frexp(amax)[1] - 1 + 127 - 7
    else:
        mant, ex = np.frexp(amax / 6.0)
        byte = np.where(mant > 0.5, ex, ex - 1) + 127
    byte = np.clip(np.where(amax > 0, byte, 1), 1, 254)
    scaled = (w * np.exp2(127.0 - byte)[:, None, :]).reshape(k, n).astype(np.float32)
    by_word = np.ascontiguousarray(scaled.reshape(k // 512, 128, 4, n).transpose(0, 1, 3, 2))
    if fmt == "e4m3":
        words = by_word.astype(ml_dtypes.float8_e4m3fn).view(np.uint8)
    else:
        c = by_word.astype(ml_dtypes.float4_e2m1fn).view(np.uint8) & 0xF
        words = c[..., 0::2] | (c[..., 1::2] << 4)
    return np.ascontiguousarray(words), np.ascontiguousarray(byte.astype(np.uint8).reshape(k // 512, 16, n))


def unpack_weight(words, scales, fmt):
    g, p, n, _ = words.shape
    if fmt == "e4m3":
        vals = np.ascontiguousarray(words).view(ml_dtypes.float8_e4m3fn).astype(np.float64)
    else:
        nib = np.empty((g, p, n, 4), np.uint8)
        nib[..., 0::2] = words & 0xF
        nib[..., 1::2] = words >> 4
        vals = E2M1[nib]
    vals = vals * np.repeat(np.exp2(scales.astype(np.float64) - 127.0), 8, axis=1)[..., None]
    return vals.transpose(0, 1, 3, 2).reshape(g * 512, n)

def pack4(w):
    words, scales = pack_weight(w, "e2m1")
    return words.reshape(words.shape[0], 128, -1), scales


def unpack4(words, scales):
    return unpack_weight(words.reshape(words.shape[0], 128, -1, 2), scales, "e2m1")


B, S, H, NH, FF = 2, 128, 1024, 8, 1024
EPS = 1e-7


def layer_norm(x, g, b):
    m = x.mean(-1, keepdims=True)
    v = ((x - m) ** 2).mean(-1, keepdims=True)
    return (x - m) / np.sqrt(v + EPS) * g + b


def setup_inputs():
    s = mx_kscale(FF)
    r = np.random.standard_normal
    ff = bf(r((B, S, FF)) * 0.65 * s)
    attn_out = bf(r((B, S, H)))
    Wf_words, Wf_scales = pack4(r((FF, H)) * 1.5 / np.sqrt(FF) / s[:, None])
    return {"ff": ff, "attn_out": attn_out,
            "Wf_words": Wf_words, "Wf_scales": Wf_scales, "b_f": bf(r(H) * 0.2),
            "ln2_g": bf(1.0 + 0.1 * r(H)), "ln2_b": bf(0.1 * r(H))}


def reference(ff, attn_out, Wf_words, Wf_scales, b_f, ln2_g, ln2_b):
    u = (mxq(f64(ff), 2, "e4m3") @ unpack4(Wf_words, Wf_scales)) + f64(b_f) + f64(attn_out)
    return layer_norm(u, f64(ln2_g), f64(ln2_b))

@@ -1,0 +1,248 @@
+from contextlib import ExitStack
+
+import concourse.mybir as mybir
+from concourse.masks import make_identity
+
+F32 = mybir.dt.float32
+BF16 = mybir.dt.bfloat16
+I32 = mybir.dt.int32
+U32 = mybir.dt.uint32
+U8 = mybir.dt.uint8
+FP8X4 = mybir.dt.float8_e4m3fn_x4
+FP4X4 = mybir.dt.float4_e2m1fn_x4
+ALU = mybir.AluOpType
+ACT = mybir.ActivationFunctionType
+
+P = 128
+PACK = 4
+K_PASS = P * PACK
+TOKEN_TILES = 2
+K = 1024
+H = 1024
+K_PASSES = K // K_PASS
+N_TILE = 512
+N_TILES = H // N_TILE
+PAIR = 2
+WORDS_PER_PASS = K_PASS // PAIR
+VECTOR_ROWS = H // (PAIR * P)
+EPS = 1e-7
+BIAS, GAIN, SHIFT = 0, 1, 2
+
+FLOPS = 2 * TOKEN_TILES * P * K * H
+
+
+def tile_disentangledattention_pc_s_kernel(
+    tc, ff, attn_out, Wf_words, Wf_scales, b_f, ln2_g, ln2_b, out
+):
+    nc = tc.nc
+    with ExitStack() as ctx:
+        keep = ctx.enter_context(tc.tile_pool(name="keep", bufs=1))
+        psum = ctx.enter_context(tc.psum_pool(name="psum", bufs=1))
+
+        vector_rows = keep.tile([P, 3, PAIR * P], BF16, name="vector_rows")
+        nc.vector.memset(vector_rows[:], 0.0)
+        w_scales = keep.tile([P, K_PASSES, H], U8, name="w_scales", align_bytes=64)
+        nc.vector.memset(w_scales[:].bitcast(I32), 0)
+        eps = keep.tile([P, 1], F32, name="eps")
+        nc.vector.memset(eps[:], EPS)
+        identity = keep.tile([P, P], F32, name="identity")
+        make_identity(nc, identity[:])
+        table_warmer = keep.tile([P, 1], F32, name="table_warmer")
+        nc.scalar.activation(out=table_warmer[:], in_=eps[:], func=ACT.Sqrt)
+
+        ff_sb = [keep.tile([P, K], BF16, name="ff_sb%d" % i) for i in range(TOKEN_TILES)]
+        attn_sb = [keep.tile([P, H], BF16, name="attn_sb%d" % i) for i in range(TOKEN_TILES)]
+        w_words = keep.tile([P, K_PASSES, 2 * H], U8, name="w_words", align_bytes=64)
+
+        def load_vector(queue, v, vector):
+            queue.dma_start(
+                out=vector_rows[0:VECTOR_ROWS, v, :],
+                in_=vector.rearrange("(c w) -> c w", w=PAIR * P),
+            )
+
+        load_vector(nc.scalar, BIAS, b_f)
+        load_vector(nc.gpsimd, GAIN, ln2_g)
+        load_vector(nc.gpsimd, SHIFT, ln2_b)
+
+        nc.sync.dma_start(out=ff_sb[0][:], in_=ff[0])
+        for quadrant in range(4):
+            nc.sync.dma_start(
+                out=w_scales[32 * quadrant : 32 * quadrant + 4].bitcast(I32),
+                in_=Wf_scales[:, 4 * quadrant : 4 * quadrant + 4, :]
+                .rearrange("g r n -> r g n")
+                .bitcast(I32),
+            )
+        nc.sync.dma_start(
+            out=w_words[:].bitcast(I32), in_=Wf_words.rearrange("g p n -> p g n").bitcast(I32)
+        )
+        nc.sync.dma_start(out=ff_sb[1][:], in_=ff[1])
+        for i in range(TOKEN_TILES):
+            nc.sync.dma_start(out=attn_sb[i][:], in_=attn_out[i])
+
+        columns_ps = psum.tile([P, 3, P], F32, name="columns_ps")
+        columns_sb = keep.tile([P, 3, VECTOR_ROWS], F32, name="columns_sb")
+
+        def vector_to_columns(v):
+            nc.tensor.transpose(columns_ps[:, v, :], vector_rows[:, v, :].bitcast(F32), identity[:])
+            nc.scalar.copy(out=columns_sb[:, v, :], in_=columns_ps[:, v, 0:VECTOR_ROWS])
+
+        def spread_columns(v, spread_ps):
+            for c in range(VECTOR_ROWS):
+                nc.tensor.transpose(
+                    spread_ps[:, c * P : (c + 1) * P],
+                    columns_sb[:, v, c : c + 1].to_broadcast([P, P]),
+                    identity[:],
+                )
+
+        ff_codes = [
+            keep.tile([P, K_PASSES * P], U32, name="ff_codes%d" % i, align_bytes=64)
+            for i in range(TOKEN_TILES)
+        ]
+        ff_scales = [
+            keep.tile([P, K_PASSES * P], U8, name="ff_scales%d" % i, align_bytes=64)
+            for i in range(TOKEN_TILES)
+        ]
+        ff_grouped = [
+            keep.tile([P, K_PASSES, P, PACK], BF16, name="ff_grouped%d" % i, align_bytes=64)
+            for i in range(TOKEN_TILES)
+        ]
+
+        def transpose_ff(i):
+            ff_t = psum.tile([P, K_PASSES, PAIR, P], F32, name="ff_t%d" % i, tag="swap%d" % i)
+            words = ff_sb[i][:].bitcast(F32)
+            for g in range(K_PASSES):
+                for u in range(PAIR):
+                    nc.tensor.transpose(
+                        ff_t[:, g, u, :],
+                        words[:, WORDS_PER_PASS * g + u : WORDS_PER_PASS * (g + 1) : PAIR],
+                        identity[:],
+                    )
+            nc.scalar.copy(
+                out=ff_grouped[i][:].bitcast(F32), in_=ff_t[:].rearrange("p g u r -> p g r u")
+            )
+
+        def quantise_ff(i):
+            nc.vector.quantize_mx(
+                out=ff_codes[i][:].bitcast(FP8X4),
+                scales=ff_scales[i][:],
+                in_=ff_grouped[i][:].rearrange("p g r t -> p (g r t)"),
+            )
+
+        product = [
+            [psum.tile([P, N_TILE], F32, name="product%d%d" % (i, n)) for n in range(N_TILES)]
+            for i in range(TOKEN_TILES)
+        ]
+
+        def multiply(i):
+            for n in range(N_TILES):
+                for g in range(K_PASSES):
+                    nc.tensor.matmul_mx(
+                        out=product[i][n][:],
+                        lhsT=ff_codes[i][:, g * P : (g + 1) * P].bitcast(FP8X4),
+                        lhsT_scale=ff_scales[i][:, g * P : (g + 1) * P],
+                        rhs=w_words[:, g, 2 * N_TILE * n : 2 * N_TILE * (n + 1)].bitcast(FP4X4),
+                        rhs_scale=w_scales[:, g, N_TILE * n : N_TILE * (n + 1)],
+                        start=(g == 0),
+                        stop=(g == K_PASSES - 1),
+                    )
+
+        residual = [keep.tile([P, H], F32, name="residual%d" % i) for i in range(TOKEN_TILES)]
+        u = [keep.tile([P, H], F32, name="u%d" % i) for i in range(TOKEN_TILES)]
+        squares = [keep.tile([P, H], BF16, name="squares%d" % i) for i in range(TOKEN_TILES)]
+        scaled = [keep.tile([P, H], F32, name="scaled%d" % i) for i in range(TOKEN_TILES)]
+        result = [keep.tile([P, H], F32, name="result%d" % i) for i in range(TOKEN_TILES)]
+        sums = [keep.tile([P, N_TILES], F32, name="sums%d" % i) for i in range(TOKEN_TILES)]
+        neg_mean = [keep.tile([P, 1], F32, name="neg_mean%d" % i) for i in range(TOKEN_TILES)]
+        sum_sq = [keep.tile([P, 1], F32, name="sum_sq%d" % i) for i in range(TOKEN_TILES)]
+        std = [keep.tile([P, 1], F32, name="std%d" % i) for i in range(TOKEN_TILES)]
+        rstd = [keep.tile([P, 1], F32, name="rstd%d" % i) for i in range(TOKEN_TILES)]
+
+        def add_bias_to_residual(i):
+            nc.vector.tensor_tensor(
+                out=residual[i][:], in0=attn_sb[i][:], in1=bias_ps[:].bitcast(BF16), op=ALU.add
+            )
+
+        def add_residual_and_mean(i):
+            for n in range(N_TILES):
+                cols = slice(N_TILE * n, N_TILE * (n + 1))
+                nc.vector.scalar_tensor_tensor(
+                    out=u[i][:, cols],
+                    in0=product[i][n][:],
+                    scalar=1.0,
+                    in1=residual[i][:, cols],
+                    op0=ALU.mult,
+                    op1=ALU.add,
+                    accum_out=sums[i][:, n : n + 1],
+                )
+            nc.vector.tensor_scalar(
+                out=neg_mean[i][:],
+                in0=sums[i][:, 0:1],
+                scalar1=sums[i][:, 1:2],
+                scalar2=-1.0 / H,
+                op0=ALU.add,
+                op1=ALU.mult,
+            )
+
+        def deviation(i):
+            nc.scalar.activation(
+                out=squares[i][:],
+                in_=u[i][:],
+                func=ACT.Square,
+                bias=neg_mean[i][:],
+                scale=1.0,
+                accum_out=sum_sq[i][:],
+            )
+            nc.scalar.activation(
+                out=std[i][:], in_=sum_sq[i][:], func=ACT.Sqrt, bias=eps[:], scale=1.0 / H
+            )
+
+        def centre_and_gain(i):
+            nc.vector.scalar_tensor_tensor(
+                out=scaled[i][:],
+                in0=u[i][:],
+                scalar=neg_mean[i][:],
+                in1=gain_ps[:].bitcast(BF16),
+                op0=ALU.add,
+                op1=ALU.mult,
+            )
+
+        def normalise_shift_store(i):
+            nc.vector.reciprocal(out=rstd[i][:], in_=std[i][:])
+            for n in range(N_TILES):
+                cols = slice(N_TILE * n, N_TILE * (n + 1))
+                nc.vector.scalar_tensor_tensor(
+                    out=result[i][:, cols],
+                    in0=scaled[i][:, cols],
+                    scalar=rstd[i][:],
+                    in1=shift_ps[:].bitcast(BF16)[:, cols],
+                    op0=ALU.mult,
+                    op1=ALU.add,
+                )
+                nc.sync.dma_start(out=out[i][:, cols], in_=result[i][:, cols])
+
+        vector_to_columns(BIAS)
+        transpose_ff(0)
+        bias_ps = psum.tile([P, H // PAIR], F32, name="bias_ps")
+        spread_columns(BIAS, bias_ps)
+        vector_to_columns(GAIN)
+        quantise_ff(0)
+        transpose_ff(1)
+        gain_ps = psum.tile([P, H // PAIR], F32, name="gain_ps", tag="swap0")
+        spread_columns(GAIN, gain_ps)
+        vector_to_columns(SHIFT)
+        multiply(0)
+        add_bias_to_residual(0)
+        quantise_ff(1)
+        shift_ps = psum.tile([P, H // PAIR], F32, name="shift_ps", tag="swap1")
+        spread_columns(SHIFT, shift_ps)
+        multiply(1)
+
+        add_residual_and_mean(0)
+        deviation(0)
+        centre_and_gain(0)
+        add_bias_to_residual(1)
+        add_residual_and_mean(1)
+        deviation(1)
+        normalise_shift_store(0)
+        centre_and_gain(1)
+        normalise_shift_store(1)

@@ -36,17 +36,18 @@ def tile_disentangledattention_pc_s_kernel(
 ):
     nc = tc.nc
     with ExitStack() as ctx:
+        ctx.enter_context(tc.manual_schedule())
         keep = ctx.enter_context(tc.tile_pool(name="keep", bufs=1))
         psum = ctx.enter_context(tc.psum_pool(name="psum", bufs=1))
 
         vector_rows = keep.tile([P, 3, PAIR * P], BF16, name="vector_rows")
         nc.vector.memset(vector_rows[:], 0.0)
+        identity = keep.tile([P, P], F32, name="identity")
+        nc.vector.memset(identity[:], 0.0)
         w_scales = keep.tile([P, K_PASSES, H], U8, name="w_scales", align_bytes=64)
         nc.vector.memset(w_scales[:].bitcast(I32), 0)
         eps = keep.tile([P, 1], F32, name="eps")
         nc.vector.memset(eps[:], EPS)
-        identity = keep.tile([P, P], F32, name="identity")
-        make_identity(nc, identity[:])
         table_warmer = keep.tile([P, 1], F32, name="table_warmer")
         nc.scalar.activation(out=table_warmer[:], in_=eps[:], func=ACT.Sqrt)
 
@@ -54,17 +55,20 @@ def tile_disentangledattention_pc_s_kernel(
         attn_sb = [keep.tile([P, H], BF16, name="attn_sb%d" % i) for i in range(TOKEN_TILES)]
         w_words = keep.tile([P, K_PASSES, 2 * H], U8, name="w_words", align_bytes=64)
 
-        def load_vector(queue, v, vector):
-            queue.dma_start(
+        def load_vector(v, vector):
+            nc.gpsimd.dma_start(
                 out=vector_rows[0:VECTOR_ROWS, v, :],
                 in_=vector.rearrange("(c w) -> c w", w=PAIR * P),
             )
 
-        load_vector(nc.scalar, BIAS, b_f)
-        load_vector(nc.gpsimd, GAIN, ln2_g)
-        load_vector(nc.gpsimd, SHIFT, ln2_b)
+        load_vector(BIAS, b_f)
+        make_identity(nc, identity[:], nomemset=True)
+        load_vector(GAIN, ln2_g)
+        load_vector(SHIFT, ln2_b)
 
         nc.sync.dma_start(out=ff_sb[0][:], in_=ff[0])
+        nc.sync.dma_start(out=attn_sb[0][:], in_=attn_out[0])
+        nc.sync.dma_start(out=ff_sb[1][:], in_=ff[1])
         for quadrant in range(4):
             nc.sync.dma_start(
                 out=w_scales[32 * quadrant : 32 * quadrant + 4].bitcast(I32),
@@ -75,16 +79,14 @@ def tile_disentangledattention_pc_s_kernel(
         nc.sync.dma_start(
             out=w_words[:].bitcast(I32), in_=Wf_words.rearrange("g p n -> p g n").bitcast(I32)
         )
-        nc.sync.dma_start(out=ff_sb[1][:], in_=ff[1])
-        for i in range(TOKEN_TILES):
-            nc.sync.dma_start(out=attn_sb[i][:], in_=attn_out[i])
+        nc.sync.dma_start(out=attn_sb[1][:], in_=attn_out[1])
 
         columns_ps = psum.tile([P, 3, P], F32, name="columns_ps")
-        columns_sb = keep.tile([P, 3, VECTOR_ROWS], F32, name="columns_sb")
+        columns_sb = keep.tile([P, 3, 8], F32, name="columns_sb")
 
-        def vector_to_columns(v):
+        def vector_to_columns(v, copy_out):
             nc.tensor.transpose(columns_ps[:, v, :], vector_rows[:, v, :].bitcast(F32), identity[:])
-            nc.scalar.copy(out=columns_sb[:, v, :], in_=columns_ps[:, v, 0:VECTOR_ROWS])
+            copy_out(out=columns_sb[:, v, 0:VECTOR_ROWS], in_=columns_ps[:, v, 0:VECTOR_ROWS])
 
         def spread_columns(v, spread_ps):
             for c in range(VECTOR_ROWS):
@@ -157,10 +159,15 @@ def tile_disentangledattention_pc_s_kernel(
         std = [keep.tile([P, 1], F32, name="std%d" % i) for i in range(TOKEN_TILES)]
         rstd = [keep.tile([P, 1], F32, name="rstd%d" % i) for i in range(TOKEN_TILES)]
 
-        def add_bias_to_residual(i):
-            nc.vector.tensor_tensor(
-                out=residual[i][:], in0=attn_sb[i][:], in1=bias_ps[:].bitcast(BF16), op=ALU.add
-            )
+        def add_bias_to_residual(i, engine, bias_words):
+            for n in range(N_TILES):
+                cols = slice(N_TILE * n, N_TILE * (n + 1))
+                engine.tensor_tensor(
+                    out=residual[i][:, cols],
+                    in0=attn_sb[i][:, cols],
+                    in1=bias_words[:].bitcast(BF16)[:, cols],
+                    op=ALU.add,
+                )
 
         def add_residual_and_mean(i):
             for n in range(N_TILES):
@@ -220,29 +227,31 @@ def tile_disentangledattention_pc_s_kernel(
                 )
                 nc.sync.dma_start(out=out[i][:, cols], in_=result[i][:, cols])
 
-        vector_to_columns(BIAS)
         transpose_ff(0)
+        vector_to_columns(BIAS, nc.vector.tensor_copy)
         bias_ps = psum.tile([P, H // PAIR], F32, name="bias_ps")
         spread_columns(BIAS, bias_ps)
-        vector_to_columns(GAIN)
-        quantise_ff(0)
+        bias_sb = keep.tile([P, H // PAIR], F32, name="bias_sb")
+        nc.scalar.copy(out=bias_sb[:], in_=bias_ps[:])
         transpose_ff(1)
+        quantise_ff(0)
+        add_bias_to_residual(0, nc.vector, bias_ps)
+        vector_to_columns(GAIN, nc.scalar.copy)
+        multiply(0)
+        quantise_ff(1)
         gain_ps = psum.tile([P, H // PAIR], F32, name="gain_ps", tag="swap0")
         spread_columns(GAIN, gain_ps)
-        vector_to_columns(SHIFT)
-        multiply(0)
-        add_bias_to_residual(0)
-        quantise_ff(1)
-        shift_ps = psum.tile([P, H // PAIR], F32, name="shift_ps", tag="swap1")
-        spread_columns(SHIFT, shift_ps)
         multiply(1)
+        add_bias_to_residual(1, nc.gpsimd, bias_sb)
 
         add_residual_and_mean(0)
         deviation(0)
         centre_and_gain(0)
-        add_bias_to_residual(1)
+        vector_to_columns(SHIFT, nc.scalar.copy)
+        shift_ps = psum.tile([P, H // PAIR], F32, name="shift_ps", tag="swap1")
+        spread_columns(SHIFT, shift_ps)
         add_residual_and_mean(1)
         deviation(1)
-        normalise_shift_store(0)
         centre_and_gain(1)
+        normalise_shift_store(0)
         normalise_shift_store(1)

@@ -24,7 +24,7 @@ N_TILE = 512
 N_TILES = H // N_TILE
 PAIR = 2
 WORDS_PER_PASS = K_PASS // PAIR
-VECTOR_ROWS = H // (PAIR * P)
+VECTOR_WORDS = H // (PAIR * P)
 EPS = 1e-7
 BIAS, GAIN, SHIFT = 0, 1, 2
 
@@ -36,39 +36,42 @@ def tile_disentangledattention_pc_s_kernel(
 ):
     nc = tc.nc
     with ExitStack() as ctx:
-        ctx.enter_context(tc.manual_schedule())
         keep = ctx.enter_context(tc.tile_pool(name="keep", bufs=1))
         psum = ctx.enter_context(tc.psum_pool(name="psum", bufs=1))
 
-        vector_rows = keep.tile([P, 3, PAIR * P], BF16, name="vector_rows")
-        nc.vector.memset(vector_rows[:], 0.0)
         identity = keep.tile([P, P], F32, name="identity")
         nc.vector.memset(identity[:], 0.0)
         w_scales = keep.tile([P, K_PASSES, H], U8, name="w_scales", align_bytes=64)
         nc.vector.memset(w_scales[:].bitcast(I32), 0)
         eps = keep.tile([P, 1], F32, name="eps")
         nc.vector.memset(eps[:], EPS)
-        table_warmer = keep.tile([P, 1], F32, name="table_warmer")
-        nc.scalar.activation(out=table_warmer[:], in_=eps[:], func=ACT.Sqrt)
 
         ff_sb = [keep.tile([P, K], BF16, name="ff_sb%d" % i) for i in range(TOKEN_TILES)]
         attn_sb = [keep.tile([P, H], BF16, name="attn_sb%d" % i) for i in range(TOKEN_TILES)]
         w_words = keep.tile([P, K_PASSES, 2 * H], U8, name="w_words", align_bytes=64)
 
+        vector_words = keep.tile([P, 3, 2 * VECTOR_WORDS * PAIR], BF16, name="vector_words")
+
         def load_vector(v, vector):
-            nc.gpsimd.dma_start(
-                out=vector_rows[0:VECTOR_ROWS, v, :],
-                in_=vector.rearrange("(c w) -> c w", w=PAIR * P),
+            nc.scalar.dma_start(
+                out=vector_words[:, v, 0 : VECTOR_WORDS * PAIR],
+                in_=vector.rearrange("(p w) -> p w", w=VECTOR_WORDS * PAIR),
             )
 
         load_vector(BIAS, b_f)
-        make_identity(nc, identity[:], nomemset=True)
         load_vector(GAIN, ln2_g)
         load_vector(SHIFT, ln2_b)
+        make_identity(nc, identity[:], nomemset=True)
+        table_warmer = keep.tile([P, 1], F32, name="table_warmer")
+        nc.scalar.activation(out=table_warmer[:], in_=eps[:], func=ACT.Sqrt)
 
         nc.sync.dma_start(out=ff_sb[0][:], in_=ff[0])
         nc.sync.dma_start(out=attn_sb[0][:], in_=attn_out[0])
+        nc.sync.dma_start(out=attn_sb[1][:], in_=attn_out[1])
         nc.sync.dma_start(out=ff_sb[1][:], in_=ff[1])
+        nc.sync.dma_start(
+            out=w_words[:].bitcast(I32), in_=Wf_words.rearrange("g p n -> p g n").bitcast(I32)
+        )
         for quadrant in range(4):
             nc.sync.dma_start(
                 out=w_scales[32 * quadrant : 32 * quadrant + 4].bitcast(I32),
@@ -76,23 +79,13 @@ def tile_disentangledattention_pc_s_kernel(
                 .rearrange("g r n -> r g n")
                 .bitcast(I32),
             )
-        nc.sync.dma_start(
-            out=w_words[:].bitcast(I32), in_=Wf_words.rearrange("g p n -> p g n").bitcast(I32)
-        )
-        nc.sync.dma_start(out=attn_sb[1][:], in_=attn_out[1])
 
-        columns_ps = psum.tile([P, 3, P], F32, name="columns_ps")
-        columns_sb = keep.tile([P, 3, 8], F32, name="columns_sb")
-
-        def vector_to_columns(v, copy_out):
-            nc.tensor.transpose(columns_ps[:, v, :], vector_rows[:, v, :].bitcast(F32), identity[:])
-            copy_out(out=columns_sb[:, v, 0:VECTOR_ROWS], in_=columns_ps[:, v, 0:VECTOR_ROWS])
-
-        def spread_columns(v, spread_ps):
-            for c in range(VECTOR_ROWS):
+        def spread_vector(v, spread_ps):
+            words = vector_words[:, v, 0 : VECTOR_WORDS * PAIR].bitcast(F32)
+            for c in range(VECTOR_WORDS):
                 nc.tensor.transpose(
-                    spread_ps[:, c * P : (c + 1) * P],
-                    columns_sb[:, v, c : c + 1].to_broadcast([P, P]),
+                    spread_ps[:, c : H // PAIR : VECTOR_WORDS],
+                    words[:, c : c + 1].to_broadcast([P, P]),
                     identity[:],
                 )
 
@@ -110,7 +103,7 @@ def tile_disentangledattention_pc_s_kernel(
         ]
 
         def transpose_ff(i):
-            ff_t = psum.tile([P, K_PASSES, PAIR, P], F32, name="ff_t%d" % i, tag="swap%d" % i)
+            ff_t = psum.tile([P, K_PASSES, PAIR, P], F32, name="ff_t%d" % i, tag="ff_t")
             words = ff_sb[i][:].bitcast(F32)
             for g in range(K_PASSES):
                 for u in range(PAIR):
@@ -227,29 +220,24 @@ def tile_disentangledattention_pc_s_kernel(
                 )
                 nc.sync.dma_start(out=out[i][:, cols], in_=result[i][:, cols])
 
-        transpose_ff(0)
-        vector_to_columns(BIAS, nc.vector.tensor_copy)
         bias_ps = psum.tile([P, H // PAIR], F32, name="bias_ps")
-        spread_columns(BIAS, bias_ps)
-        bias_sb = keep.tile([P, H // PAIR], F32, name="bias_sb")
-        nc.scalar.copy(out=bias_sb[:], in_=bias_ps[:])
-        transpose_ff(1)
-        quantise_ff(0)
+        gain_ps = psum.tile([P, H // PAIR], F32, name="gain_ps")
+        shift_ps = psum.tile([P, H // PAIR], F32, name="shift_ps")
+        spread_vector(BIAS, bias_ps)
+        transpose_ff(0)
         add_bias_to_residual(0, nc.vector, bias_ps)
-        vector_to_columns(GAIN, nc.scalar.copy)
-        multiply(0)
+        quantise_ff(0)
+        transpose_ff(1)
+        add_bias_to_residual(1, nc.vector, bias_ps)
         quantise_ff(1)
-        gain_ps = psum.tile([P, H // PAIR], F32, name="gain_ps", tag="swap0")
-        spread_columns(GAIN, gain_ps)
+        spread_vector(GAIN, gain_ps)
+        multiply(0)
+        spread_vector(SHIFT, shift_ps)
         multiply(1)
-        add_bias_to_residual(1, nc.gpsimd, bias_sb)
 
         add_residual_and_mean(0)
         deviation(0)
         centre_and_gain(0)
-        vector_to_columns(SHIFT, nc.scalar.copy)
-        shift_ps = psum.tile([P, H // PAIR], F32, name="shift_ps", tag="swap1")
-        spread_columns(SHIFT, shift_ps)
         add_residual_and_mean(1)
         deviation(1)
         centre_and_gain(1)

@@ -38,13 +38,14 @@ def tile_disentangledattention_pc_s_kernel(
     with ExitStack() as ctx:
         keep = ctx.enter_context(tc.tile_pool(name="keep", bufs=1))
         psum = ctx.enter_context(tc.psum_pool(name="psum", bufs=1))
+        ctx.enter_context(tc.manual_schedule())
 
-        identity = keep.tile([P, P], F32, name="identity")
-        nc.vector.memset(identity[:], 0.0)
         w_scales = keep.tile([P, K_PASSES, H], U8, name="w_scales", align_bytes=64)
         nc.vector.memset(w_scales[:].bitcast(I32), 0)
         eps = keep.tile([P, 1], F32, name="eps")
         nc.vector.memset(eps[:], EPS)
+        identity = keep.tile([P, P], F32, name="identity")
+        make_identity(nc, identity[:])
 
         ff_sb = [keep.tile([P, K], BF16, name="ff_sb%d" % i) for i in range(TOKEN_TILES)]
         attn_sb = [keep.tile([P, H], BF16, name="attn_sb%d" % i) for i in range(TOKEN_TILES)]
@@ -58,17 +59,10 @@ def tile_disentangledattention_pc_s_kernel(
                 in_=vector.rearrange("(p w) -> p w", w=VECTOR_WORDS * PAIR),
             )
 
-        load_vector(BIAS, b_f)
-        load_vector(GAIN, ln2_g)
-        load_vector(SHIFT, ln2_b)
-        make_identity(nc, identity[:], nomemset=True)
-        table_warmer = keep.tile([P, 1], F32, name="table_warmer")
-        nc.scalar.activation(out=table_warmer[:], in_=eps[:], func=ACT.Sqrt)
-
         nc.sync.dma_start(out=ff_sb[0][:], in_=ff[0])
-        nc.sync.dma_start(out=attn_sb[0][:], in_=attn_out[0])
-        nc.sync.dma_start(out=attn_sb[1][:], in_=attn_out[1])
+        load_vector(BIAS, b_f)
         nc.sync.dma_start(out=ff_sb[1][:], in_=ff[1])
+        load_vector(GAIN, ln2_g)
         nc.sync.dma_start(
             out=w_words[:].bitcast(I32), in_=Wf_words.rearrange("g p n -> p g n").bitcast(I32)
         )
@@ -79,6 +73,11 @@ def tile_disentangledattention_pc_s_kernel(
                 .rearrange("g r n -> r g n")
                 .bitcast(I32),
             )
+        nc.sync.dma_start(out=attn_sb[0][:], in_=attn_out[0])
+        nc.sync.dma_start(out=attn_sb[1][:], in_=attn_out[1])
+        table_warmer = keep.tile([P, 1], F32, name="table_warmer")
+        nc.scalar.activation(out=table_warmer[:], in_=eps[:], func=ACT.Sqrt)
+        load_vector(SHIFT, ln2_b)
 
         def spread_vector(v, spread_ps):
             words = vector_words[:, v, 0 : VECTOR_WORDS * PAIR].bitcast(F32)
@@ -102,8 +101,8 @@ def tile_disentangledattention_pc_s_kernel(
             for i in range(TOKEN_TILES)
         ]
 
-        def transpose_ff(i):
-            ff_t = psum.tile([P, K_PASSES, PAIR, P], F32, name="ff_t%d" % i, tag="ff_t")
+        def transpose_ff(i, bank_tag):
+            ff_t = psum.tile([P, K_PASSES, PAIR, P], F32, name="ff_t%d" % i, tag=bank_tag)
             words = ff_sb[i][:].bitcast(F32)
             for g in range(K_PASSES):
                 for u in range(PAIR):
@@ -112,6 +111,9 @@ def tile_disentangledattention_pc_s_kernel(
                         words[:, WORDS_PER_PASS * g + u : WORDS_PER_PASS * (g + 1) : PAIR],
                         identity[:],
                     )
+            return ff_t
+
+        def group_ff(i, ff_t):
             nc.scalar.copy(
                 out=ff_grouped[i][:].bitcast(F32), in_=ff_t[:].rearrange("p g u r -> p g r u")
             )
@@ -123,16 +125,11 @@ def tile_disentangledattention_pc_s_kernel(
                 in_=ff_grouped[i][:].rearrange("p g r t -> p (g r t)"),
             )
 
-        product = [
-            [psum.tile([P, N_TILE], F32, name="product%d%d" % (i, n)) for n in range(N_TILES)]
-            for i in range(TOKEN_TILES)
-        ]
-
-        def multiply(i):
+        def multiply(i, product):
             for n in range(N_TILES):
                 for g in range(K_PASSES):
                     nc.tensor.matmul_mx(
-                        out=product[i][n][:],
+                        out=product[n][:],
                         lhsT=ff_codes[i][:, g * P : (g + 1) * P].bitcast(FP8X4),
                         lhsT_scale=ff_scales[i][:, g * P : (g + 1) * P],
                         rhs=w_words[:, g, 2 * N_TILE * n : 2 * N_TILE * (n + 1)].bitcast(FP4X4),
@@ -152,22 +149,21 @@ def tile_disentangledattention_pc_s_kernel(
         std = [keep.tile([P, 1], F32, name="std%d" % i) for i in range(TOKEN_TILES)]
         rstd = [keep.tile([P, 1], F32, name="rstd%d" % i) for i in range(TOKEN_TILES)]
 
-        def add_bias_to_residual(i, engine, bias_words):
-            for n in range(N_TILES):
-                cols = slice(N_TILE * n, N_TILE * (n + 1))
-                engine.tensor_tensor(
-                    out=residual[i][:, cols],
-                    in0=attn_sb[i][:, cols],
-                    in1=bias_words[:].bitcast(BF16)[:, cols],
-                    op=ALU.add,
-                )
+        def add_bias_to_residual(i, n, engine, bias_bf16):
+            cols = slice(N_TILE * n, N_TILE * (n + 1))
+            engine.tensor_tensor(
+                out=residual[i][:, cols],
+                in0=attn_sb[i][:, cols],
+                in1=bias_bf16[:, cols],
+                op=ALU.add,
+            )
 
-        def add_residual_and_mean(i):
+        def add_residual_and_mean(i, product):
             for n in range(N_TILES):
                 cols = slice(N_TILE * n, N_TILE * (n + 1))
                 nc.vector.scalar_tensor_tensor(
                     out=u[i][:, cols],
-                    in0=product[i][n][:],
+                    in0=product[n][:],
                     scalar=1.0,
                     in1=residual[i][:, cols],
                     op0=ALU.mult,
@@ -223,22 +219,35 @@ def tile_disentangledattention_pc_s_kernel(
         bias_ps = psum.tile([P, H // PAIR], F32, name="bias_ps")
         gain_ps = psum.tile([P, H // PAIR], F32, name="gain_ps")
         shift_ps = psum.tile([P, H // PAIR], F32, name="shift_ps")
+        bias_sb = keep.tile([P, H // PAIR], F32, name="bias_sb")
+
         spread_vector(BIAS, bias_ps)
-        transpose_ff(0)
-        add_bias_to_residual(0, nc.vector, bias_ps)
+        nc.scalar.copy(out=bias_sb[:], in_=bias_ps[:])
+        ff_t0 = transpose_ff(0, "ff_t")
+        group_ff(0, ff_t0)
+        ff_t1 = transpose_ff(1, "product11")
+        group_ff(1, ff_t1)
         quantise_ff(0)
-        transpose_ff(1)
-        add_bias_to_residual(1, nc.vector, bias_ps)
         quantise_ff(1)
         spread_vector(GAIN, gain_ps)
-        multiply(0)
-        spread_vector(SHIFT, shift_ps)
-        multiply(1)
 
-        add_residual_and_mean(0)
+        product = [
+            [psum.tile([P, N_TILE], F32, name="product%d%d" % (i, n)) for n in range(N_TILES)]
+            for i in range(TOKEN_TILES)
+        ]
+        multiply(0, product[0])
+        multiply(1, product[1])
+        spread_vector(SHIFT, shift_ps)
+
+        add_bias_to_residual(0, 0, nc.vector, bias_ps[:].bitcast(BF16))
+        add_bias_to_residual(0, 1, nc.gpsimd, bias_sb[:].bitcast(BF16))
+        add_bias_to_residual(1, 0, nc.gpsimd, bias_sb[:].bitcast(BF16))
+        add_bias_to_residual(1, 1, nc.gpsimd, bias_sb[:].bitcast(BF16))
+
+        add_residual_and_mean(0, product[0])
         deviation(0)
         centre_and_gain(0)
-        add_residual_and_mean(1)
+        add_residual_and_mean(1, product[1])
         deviation(1)
         centre_and_gain(1)
         normalise_shift_store(0)

@@ -40,6 +40,18 @@ def tile_disentangledattention_pc_s_kernel(
         psum = ctx.enter_context(tc.psum_pool(name="psum", bufs=1))
         ctx.enter_context(tc.manual_schedule())
 
+        warm_src = keep.tile([P, P], F32, name="warm_src")
+        nc.gpsimd.memset(warm_src[:], 0.0)
+        warm_ps = psum.tile([P, P], F32, name="warm_ps", tag="product10")
+
+        def keep_warm(count):
+            for unused in range(count):
+                nc.tensor.matmul(
+                    warm_ps[:], lhsT=warm_src[:], rhs=warm_src[:], start=True, stop=True
+                )
+
+        keep_warm(3)
+
         w_scales = keep.tile([P, K_PASSES, H], U8, name="w_scales", align_bytes=64)
         nc.vector.memset(w_scales[:].bitcast(I32), 0)
         eps = keep.tile([P, 1], F32, name="eps")
@@ -222,14 +234,18 @@ def tile_disentangledattention_pc_s_kernel(
         bias_sb = keep.tile([P, H // PAIR], F32, name="bias_sb")
 
         spread_vector(BIAS, bias_ps)
+        keep_warm(1)
         nc.scalar.copy(out=bias_sb[:], in_=bias_ps[:])
         ff_t0 = transpose_ff(0, "ff_t")
+        keep_warm(1)
         group_ff(0, ff_t0)
         ff_t1 = transpose_ff(1, "product11")
+        keep_warm(1)
         group_ff(1, ff_t1)
         quantise_ff(0)
         quantise_ff(1)
         spread_vector(GAIN, gain_ps)
+        keep_warm(2)
 
         product = [
             [psum.tile([P, N_TILE], F32, name="product%d%d" % (i, n)) for n in range(N_TILES)]

@@ -137,6 +137,13 @@ def tile_disentangledattention_pc_s_kernel(
                 in_=ff_grouped[i][:].rearrange("p g r t -> p (g r t)"),
             )
 
+        def quantise_ff_pass(i, g):
+            nc.vector.quantize_mx(
+                out=ff_codes[i][:, g * P : (g + 1) * P].bitcast(FP8X4),
+                scales=ff_scales[i][:, g * P : (g + 1) * P],
+                in_=ff_grouped[i][:, g].rearrange("p r t -> p (r t)"),
+            )
+
         def multiply(i, product):
             for n in range(N_TILES):
                 for g in range(K_PASSES):
@@ -170,18 +177,19 @@ def tile_disentangledattention_pc_s_kernel(
                 op=ALU.add,
             )
 
-        def add_residual_and_mean(i, product):
-            for n in range(N_TILES):
-                cols = slice(N_TILE * n, N_TILE * (n + 1))
-                nc.vector.scalar_tensor_tensor(
-                    out=u[i][:, cols],
-                    in0=product[n][:],
-                    scalar=1.0,
-                    in1=residual[i][:, cols],
-                    op0=ALU.mult,
-                    op1=ALU.add,
-                    accum_out=sums[i][:, n : n + 1],
-                )
+        def add_residual(i, n, product):
+            cols = slice(N_TILE * n, N_TILE * (n + 1))
+            nc.vector.scalar_tensor_tensor(
+                out=u[i][:, cols],
+                in0=product[n][:],
+                scalar=1.0,
+                in1=residual[i][:, cols],
+                op0=ALU.mult,
+                op1=ALU.add,
+                accum_out=sums[i][:, n : n + 1],
+            )
+
+        def negative_mean(i):
             nc.vector.tensor_scalar(
                 out=neg_mean[i][:],
                 in0=sums[i][:, 0:1],
@@ -214,19 +222,20 @@ def tile_disentangledattention_pc_s_kernel(
                 op1=ALU.mult,
             )
 
-        def normalise_shift_store(i):
+        def one_over_deviation(i):
             nc.vector.reciprocal(out=rstd[i][:], in_=std[i][:])
-            for n in range(N_TILES):
-                cols = slice(N_TILE * n, N_TILE * (n + 1))
-                nc.vector.scalar_tensor_tensor(
-                    out=result[i][:, cols],
-                    in0=scaled[i][:, cols],
-                    scalar=rstd[i][:],
-                    in1=shift_ps[:].bitcast(BF16)[:, cols],
-                    op0=ALU.mult,
-                    op1=ALU.add,
-                )
-                nc.sync.dma_start(out=out[i][:, cols], in_=result[i][:, cols])
+
+        def normalise_shift_store(i, n):
+            cols = slice(N_TILE * n, N_TILE * (n + 1))
+            nc.vector.scalar_tensor_tensor(
+                out=result[i][:, cols],
+                in0=scaled[i][:, cols],
+                scalar=rstd[i][:],
+                in1=shift_ps[:].bitcast(BF16)[:, cols],
+                op0=ALU.mult,
+                op1=ALU.add,
+            )
+            nc.sync.dma_start(out=out[i][:, cols], in_=result[i][:, cols])
 
         bias_ps = psum.tile([P, H // PAIR], F32, name="bias_ps")
         gain_ps = psum.tile([P, H // PAIR], F32, name="gain_ps")
@@ -243,7 +252,6 @@ def tile_disentangledattention_pc_s_kernel(
         keep_warm(1)
         group_ff(1, ff_t1)
         quantise_ff(0)
-        quantise_ff(1)
         spread_vector(GAIN, gain_ps)
         keep_warm(2)
 
@@ -252,19 +260,29 @@ def tile_disentangledattention_pc_s_kernel(
             for i in range(TOKEN_TILES)
         ]
         multiply(0, product[0])
-        multiply(1, product[1])
-        spread_vector(SHIFT, shift_ps)
 
         add_bias_to_residual(0, 0, nc.vector, bias_ps[:].bitcast(BF16))
         add_bias_to_residual(0, 1, nc.gpsimd, bias_sb[:].bitcast(BF16))
         add_bias_to_residual(1, 0, nc.gpsimd, bias_sb[:].bitcast(BF16))
         add_bias_to_residual(1, 1, nc.gpsimd, bias_sb[:].bitcast(BF16))
 
-        add_residual_and_mean(0, product[0])
+        add_residual(0, 0, product[0])
+        add_residual(0, 1, product[0])
+        quantise_ff_pass(1, 0)
+        negative_mean(0)
+        quantise_ff_pass(1, 1)
+        multiply(1, product[1])
+        spread_vector(SHIFT, shift_ps)
         deviation(0)
         centre_and_gain(0)
-        add_residual_and_mean(1, product[1])
+        add_residual(1, 0, product[1])
+        add_residual(1, 1, product[1])
+        one_over_deviation(0)
+        negative_mean(1)
         deviation(1)
+        normalise_shift_store(0, 0)
         centre_and_gain(1)
-        normalise_shift_store(0)
-        normalise_shift_store(1)
+        one_over_deviation(1)
+        normalise_shift_store(0, 1)
+        normalise_shift_store(1, 0)
+        normalise_shift_store(1, 1)

@@ -255,28 +255,27 @@ def tile_disentangledattention_pc_s_kernel(
         spread_vector(GAIN, gain_ps)
         keep_warm(2)
 
-        product = [
-            [psum.tile([P, N_TILE], F32, name="product%d%d" % (i, n)) for n in range(N_TILES)]
-            for i in range(TOKEN_TILES)
-        ]
-        multiply(0, product[0])
+        product0 = [psum.tile([P, N_TILE], F32, name="product0%d" % n) for n in range(N_TILES)]
+        multiply(0, product0)
+        keep_warm(4)
 
         add_bias_to_residual(0, 0, nc.vector, bias_ps[:].bitcast(BF16))
         add_bias_to_residual(0, 1, nc.gpsimd, bias_sb[:].bitcast(BF16))
         add_bias_to_residual(1, 0, nc.gpsimd, bias_sb[:].bitcast(BF16))
         add_bias_to_residual(1, 1, nc.gpsimd, bias_sb[:].bitcast(BF16))
 
-        add_residual(0, 0, product[0])
-        add_residual(0, 1, product[0])
+        add_residual(0, 0, product0)
+        add_residual(0, 1, product0)
         quantise_ff_pass(1, 0)
         negative_mean(0)
         quantise_ff_pass(1, 1)
-        multiply(1, product[1])
+        product1 = [psum.tile([P, N_TILE], F32, name="product1%d" % n) for n in range(N_TILES)]
+        multiply(1, product1)
         spread_vector(SHIFT, shift_ps)
         deviation(0)
         centre_and_gain(0)
-        add_residual(1, 0, product[1])
-        add_residual(1, 1, product[1])
+        add_residual(1, 0, product1)
+        add_residual(1, 1, product1)
         one_over_deviation(0)
         negative_mean(1)
         deviation(1)

@@ -88,7 +88,7 @@ def tile_disentangledattention_pc_s_kernel(
         nc.sync.dma_start(out=attn_sb[0][:], in_=attn_out[0])
         nc.sync.dma_start(out=attn_sb[1][:], in_=attn_out[1])
         table_warmer = keep.tile([P, 1], F32, name="table_warmer")
-        nc.scalar.activation(out=table_warmer[:], in_=eps[:], func=ACT.Sqrt)
+        nc.scalar.activation(out=table_warmer[:], in_=eps[:], func=ACT.Abs_reciprocal_sqrt)
         load_vector(SHIFT, ln2_b)
 
         def spread_vector(v, spread_ps):
@@ -165,7 +165,6 @@ def tile_disentangledattention_pc_s_kernel(
         sums = [keep.tile([P, N_TILES], F32, name="sums%d" % i) for i in range(TOKEN_TILES)]
         neg_mean = [keep.tile([P, 1], F32, name="neg_mean%d" % i) for i in range(TOKEN_TILES)]
         sum_sq = [keep.tile([P, 1], F32, name="sum_sq%d" % i) for i in range(TOKEN_TILES)]
-        std = [keep.tile([P, 1], F32, name="std%d" % i) for i in range(TOKEN_TILES)]
         rstd = [keep.tile([P, 1], F32, name="rstd%d" % i) for i in range(TOKEN_TILES)]
 
         def add_bias_to_residual(i, n, engine, bias_bf16):
@@ -209,7 +208,11 @@ def tile_disentangledattention_pc_s_kernel(
                 accum_out=sum_sq[i][:],
             )
             nc.scalar.activation(
-                out=std[i][:], in_=sum_sq[i][:], func=ACT.Sqrt, bias=eps[:], scale=1.0 / H
+                out=rstd[i][:],
+                in_=sum_sq[i][:],
+                func=ACT.Abs_reciprocal_sqrt,
+                bias=eps[:],
+                scale=1.0 / H,
             )
 
         def centre_and_gain(i):
@@ -222,8 +225,22 @@ def tile_disentangledattention_pc_s_kernel(
                 op1=ALU.mult,
             )
 
-        def one_over_deviation(i):
-            nc.vector.reciprocal(out=rstd[i][:], in_=std[i][:])
+        normalised = keep.tile([P, H], F32, name="normalised")
+
+        def normalise_on_scalar(i, n):
+            cols = slice(N_TILE * n, N_TILE * (n + 1))
+            nc.scalar.activation(
+                out=normalised[:, cols], in_=scaled[i][:, cols], func=ACT.Copy, scale=rstd[i][:]
+            )
+
+        def shift_on_gpsimd(i, n):
+            cols = slice(N_TILE * n, N_TILE * (n + 1))
+            nc.gpsimd.tensor_tensor(
+                out=result[i][:, cols],
+                in0=normalised[:, cols],
+                in1=shift_sb[:].bitcast(BF16)[:, cols],
+                op=ALU.add,
+            )
 
         def normalise_shift_store(i, n):
             cols = slice(N_TILE * n, N_TILE * (n + 1))
@@ -241,6 +258,7 @@ def tile_disentangledattention_pc_s_kernel(
         gain_ps = psum.tile([P, H // PAIR], F32, name="gain_ps")
         shift_ps = psum.tile([P, H // PAIR], F32, name="shift_ps")
         bias_sb = keep.tile([P, H // PAIR], F32, name="bias_sb")
+        shift_sb = keep.tile([P, H // PAIR], F32, name="shift_sb")
 
         spread_vector(BIAS, bias_ps)
         keep_warm(1)
@@ -257,7 +275,9 @@ def tile_disentangledattention_pc_s_kernel(
 
         product0 = [psum.tile([P, N_TILE], F32, name="product0%d" % n) for n in range(N_TILES)]
         multiply(0, product0)
+        spread_vector(SHIFT, shift_ps)
         keep_warm(4)
+        nc.scalar.copy(out=shift_sb[:], in_=shift_ps[:])
 
         add_bias_to_residual(0, 0, nc.vector, bias_ps[:].bitcast(BF16))
         add_bias_to_residual(0, 1, nc.gpsimd, bias_sb[:].bitcast(BF16))
@@ -271,17 +291,16 @@ def tile_disentangledattention_pc_s_kernel(
         quantise_ff_pass(1, 1)
         product1 = [psum.tile([P, N_TILE], F32, name="product1%d" % n) for n in range(N_TILES)]
         multiply(1, product1)
-        spread_vector(SHIFT, shift_ps)
         deviation(0)
         centre_and_gain(0)
+        normalise_on_scalar(0, 1)
+        shift_on_gpsimd(0, 1)
         add_residual(1, 0, product1)
         add_residual(1, 1, product1)
-        one_over_deviation(0)
         negative_mean(1)
         deviation(1)
-        normalise_shift_store(0, 0)
+        nc.scalar.dma_start(out=out[0][:, N_TILE:H], in_=result[0][:, N_TILE:H])
         centre_and_gain(1)
-        one_over_deviation(1)
-        normalise_shift_store(0, 1)
+        normalise_shift_store(0, 0)
         normalise_shift_store(1, 0)
         normalise_shift_store(1, 1)

@@ -270,13 +270,13 @@ def tile_disentangledattention_pc_s_kernel(
         keep_warm(1)
         group_ff(1, ff_t1)
         quantise_ff(0)
-        spread_vector(GAIN, gain_ps)
-        keep_warm(2)
+        keep_warm(1)
 
         product0 = [psum.tile([P, N_TILE], F32, name="product0%d" % n) for n in range(N_TILES)]
         multiply(0, product0)
+        spread_vector(GAIN, gain_ps)
         spread_vector(SHIFT, shift_ps)
-        keep_warm(4)
+        keep_warm(2)
         nc.scalar.copy(out=shift_sb[:], in_=shift_ps[:])
 
         add_bias_to_residual(0, 0, nc.vector, bias_ps[:].bitcast(BF16))

@@ -295,12 +295,12 @@ def tile_disentangledattention_pc_s_kernel(
         centre_and_gain(0)
         normalise_on_scalar(0, 1)
         shift_on_gpsimd(0, 1)
+        nc.sync.dma_start(out=out[0][:, N_TILE:H], in_=result[0][:, N_TILE:H])
         add_residual(1, 0, product1)
         add_residual(1, 1, product1)
         negative_mean(1)
         deviation(1)
-        nc.scalar.dma_start(out=out[0][:, N_TILE:H], in_=result[0][:, N_TILE:H])
-        centre_and_gain(1)
         normalise_shift_store(0, 0)
+        centre_and_gain(1)
         normalise_shift_store(1, 0)
         normalise_shift_store(1, 1)

@@ -260,12 +260,12 @@ def tile_disentangledattention_pc_s_kernel(
         bias_sb = keep.tile([P, H // PAIR], F32, name="bias_sb")
         shift_sb = keep.tile([P, H // PAIR], F32, name="shift_sb")
 
-        spread_vector(BIAS, bias_ps)
-        keep_warm(1)
-        nc.scalar.copy(out=bias_sb[:], in_=bias_ps[:])
         ff_t0 = transpose_ff(0, "ff_t")
         keep_warm(1)
         group_ff(0, ff_t0)
+        spread_vector(BIAS, bias_ps)
+        keep_warm(1)
+        nc.scalar.copy(out=bias_sb[:], in_=bias_ps[:])
         ff_t1 = transpose_ff(1, "product11")
         keep_warm(1)
         group_ff(1, ff_t1)

@@ -137,13 +137,6 @@ def tile_disentangledattention_pc_s_kernel(
                 in_=ff_grouped[i][:].rearrange("p g r t -> p (g r t)"),
             )
 
-        def quantise_ff_pass(i, g):
-            nc.vector.quantize_mx(
-                out=ff_codes[i][:, g * P : (g + 1) * P].bitcast(FP8X4),
-                scales=ff_scales[i][:, g * P : (g + 1) * P],
-                in_=ff_grouped[i][:, g].rearrange("p r t -> p (r t)"),
-            )
-
         def multiply(i, product):
             for n in range(N_TILES):
                 for g in range(K_PASSES):
@@ -167,8 +160,7 @@ def tile_disentangledattention_pc_s_kernel(
         sum_sq = [keep.tile([P, 1], F32, name="sum_sq%d" % i) for i in range(TOKEN_TILES)]
         rstd = [keep.tile([P, 1], F32, name="rstd%d" % i) for i in range(TOKEN_TILES)]
 
-        def add_bias_to_residual(i, n, engine, bias_bf16):
-            cols = slice(N_TILE * n, N_TILE * (n + 1))
+        def add_bias_to_residual(i, cols, engine, bias_bf16):
             engine.tensor_tensor(
                 out=residual[i][:, cols],
                 in0=attn_sb[i][:, cols],
@@ -242,8 +234,7 @@ def tile_disentangledattention_pc_s_kernel(
                 op=ALU.add,
             )
 
-        def normalise_shift_store(i, n):
-            cols = slice(N_TILE * n, N_TILE * (n + 1))
+        def normalise_and_shift(i, cols):
             nc.vector.scalar_tensor_tensor(
                 out=result[i][:, cols],
                 in0=scaled[i][:, cols],
@@ -252,6 +243,8 @@ def tile_disentangledattention_pc_s_kernel(
                 op0=ALU.mult,
                 op1=ALU.add,
             )
+
+        def store(i, cols):
             nc.sync.dma_start(out=out[i][:, cols], in_=result[i][:, cols])
 
         bias_ps = psum.tile([P, H // PAIR], F32, name="bias_ps")
@@ -260,47 +253,53 @@ def tile_disentangledattention_pc_s_kernel(
         bias_sb = keep.tile([P, H // PAIR], F32, name="bias_sb")
         shift_sb = keep.tile([P, H // PAIR], F32, name="shift_sb")
 
+        bias_on_psum = bias_ps[:].bitcast(BF16)
+        bias_on_sbuf = bias_sb[:].bitcast(BF16)
+        half_cols = [slice(N_TILE * n, N_TILE * (n + 1)) for n in range(N_TILES)]
+
         ff_t0 = transpose_ff(0, "ff_t")
-        keep_warm(1)
         group_ff(0, ff_t0)
-        spread_vector(BIAS, bias_ps)
-        keep_warm(1)
-        nc.scalar.copy(out=bias_sb[:], in_=bias_ps[:])
         ff_t1 = transpose_ff(1, "product11")
-        keep_warm(1)
         group_ff(1, ff_t1)
+        keep_warm(1)
+        spread_vector(BIAS, bias_ps)
+        keep_warm(2)
+        nc.scalar.copy(out=bias_sb[:], in_=bias_ps[:])
         quantise_ff(0)
         keep_warm(1)
+        quantise_ff(1)
 
         product0 = [psum.tile([P, N_TILE], F32, name="product0%d" % n) for n in range(N_TILES)]
         multiply(0, product0)
         spread_vector(GAIN, gain_ps)
-        spread_vector(SHIFT, shift_ps)
-        keep_warm(2)
-        nc.scalar.copy(out=shift_sb[:], in_=shift_ps[:])
-
-        add_bias_to_residual(0, 0, nc.vector, bias_ps[:].bitcast(BF16))
-        add_bias_to_residual(0, 1, nc.gpsimd, bias_sb[:].bitcast(BF16))
-        add_bias_to_residual(1, 0, nc.gpsimd, bias_sb[:].bitcast(BF16))
-        add_bias_to_residual(1, 1, nc.gpsimd, bias_sb[:].bitcast(BF16))
-
-        add_residual(0, 0, product0)
-        add_residual(0, 1, product0)
-        quantise_ff_pass(1, 0)
-        negative_mean(0)
-        quantise_ff_pass(1, 1)
         product1 = [psum.tile([P, N_TILE], F32, name="product1%d" % n) for n in range(N_TILES)]
         multiply(1, product1)
+        spread_vector(SHIFT, shift_ps)
+
+        add_bias_to_residual(0, half_cols[0], nc.vector, bias_on_psum)
+        add_bias_to_residual(0, half_cols[1], nc.gpsimd, bias_on_sbuf)
+        add_bias_to_residual(1, half_cols[1], nc.gpsimd, bias_on_sbuf)
+
+        add_residual(0, 0, product0)
+        add_bias_to_residual(1, slice(0, 256), nc.vector, bias_on_psum)
+        add_residual(0, 1, product0)
+        add_bias_to_residual(1, slice(256, 384), nc.vector, bias_on_psum)
+        negative_mean(0)
+        add_bias_to_residual(1, slice(384, 512), nc.vector, bias_on_psum)
         deviation(0)
+        nc.scalar.copy(out=shift_sb[:], in_=shift_ps[:])
         centre_and_gain(0)
         normalise_on_scalar(0, 1)
         shift_on_gpsimd(0, 1)
-        nc.sync.dma_start(out=out[0][:, N_TILE:H], in_=result[0][:, N_TILE:H])
+        store(0, half_cols[1])
         add_residual(1, 0, product1)
         add_residual(1, 1, product1)
+        normalise_and_shift(0, slice(0, 256))
         negative_mean(1)
         deviation(1)
-        normalise_shift_store(0, 0)
+        normalise_and_shift(0, slice(256, 512))
+        store(0, half_cols[0])
         centre_and_gain(1)
-        normalise_shift_store(1, 0)
-        normalise_shift_store(1, 1)
+        for n in range(N_TILES):
+            normalise_and_shift(1, half_cols[n])
+            store(1, half_cols[n])

@@ -158,6 +158,10 @@ def tile_disentangledattention_pc_s_kernel(
         sums = [keep.tile([P, N_TILES], F32, name="sums%d" % i) for i in range(TOKEN_TILES)]
         neg_mean = [keep.tile([P, 1], F32, name="neg_mean%d" % i) for i in range(TOKEN_TILES)]
         sum_sq = [keep.tile([P, 1], F32, name="sum_sq%d" % i) for i in range(TOKEN_TILES)]
+        half_sq = keep.tile([P, N_TILES], F32, name="half_sq")
+        first_var = keep.tile([P, 1], F32, name="first_var")
+        offset = keep.tile([P, 1], F32, name="offset")
+        neg_rest = keep.tile([P, 1], F32, name="neg_rest")
         rstd = [keep.tile([P, 1], F32, name="rstd%d" % i) for i in range(TOKEN_TILES)]
 
         def add_bias_to_residual(i, cols, engine, bias_bf16):
@@ -207,30 +211,101 @@ def tile_disentangledattention_pc_s_kernel(
                 scale=1.0 / H,
             )
 
-        def centre_and_gain(i):
+        def half_squares(i, n):
+            cols = slice(N_TILE * n, N_TILE * (n + 1))
+            nc.scalar.activation(
+                out=squares[i][:, cols],
+                in_=u[i][:, cols],
+                func=ACT.Square,
+                bias=sums[i][:, 0:1],
+                scale=-float(N_TILE),
+                accum_out=half_sq[:, n : n + 1],
+            )
+
+        def first_half_variance(i):
+            half_squares(i, 0)
+            nc.scalar.activation(
+                out=first_var[:],
+                in_=half_sq[:, 0:1],
+                func=ACT.Identity,
+                bias=eps[:],
+                scale=1.0 / (H * N_TILE * N_TILE),
+            )
+
+        def mean_offset(i):
+            nc.vector.tensor_scalar(
+                out=offset[:],
+                in0=sums[i][:, 1:2],
+                scalar1=sums[i][:, 0:1],
+                scalar2=1.0 / H,
+                op0=ALU.subtract,
+                op1=ALU.mult,
+            )
+
+        def offset_less_first_half(i):
+            nc.vector.tensor_scalar(
+                out=neg_rest[:],
+                in0=offset[:],
+                scalar1=offset[:],
+                scalar2=first_var[:],
+                op0=ALU.mult,
+                op1=ALU.subtract,
+            )
+
+        def deviation_from_halves(i):
+            nc.scalar.activation(
+                out=rstd[i][:],
+                in_=half_sq[:, 1:2],
+                func=ACT.Abs_reciprocal_sqrt,
+                bias=neg_rest[:],
+                scale=-1.0 / (H * N_TILE * N_TILE),
+            )
+
+        def centre_and_gain(i, cols):
             nc.vector.scalar_tensor_tensor(
-                out=scaled[i][:],
-                in0=u[i][:],
+                out=scaled[i][:, cols],
+                in0=u[i][:, cols],
                 scalar=neg_mean[i][:],
-                in1=gain_ps[:].bitcast(BF16),
+                in1=gain_ps[:].bitcast(BF16)[:, cols],
                 op0=ALU.add,
                 op1=ALU.mult,
             )
 
-        normalised = keep.tile([P, H], F32, name="normalised")
+        centred = keep.tile([P, N_TILE], F32, name="centred")
 
-        def normalise_on_scalar(i, n):
+        def centre_and_gain_on_gpsimd(i, n):
             cols = slice(N_TILE * n, N_TILE * (n + 1))
-            nc.scalar.activation(
-                out=normalised[:, cols], in_=scaled[i][:, cols], func=ACT.Copy, scale=rstd[i][:]
+            nc.gpsimd.tensor_scalar(
+                out=centred[:],
+                in0=u[i][:, cols],
+                scalar1=neg_mean[i][:],
+                scalar2=1.0,
+                op0=ALU.add,
+                op1=ALU.mult,
+            )
+            nc.gpsimd.tensor_tensor(
+                out=scaled[i][:, cols],
+                in0=centred[:],
+                in1=gain_sb[:].bitcast(BF16),
+                op=ALU.mult,
             )
 
-        def shift_on_gpsimd(i, n):
+        normalised = keep.tile([P, N_TILE], F32, name="normalised")
+
+        def normalise_and_shift_on_gpsimd(i, n):
             cols = slice(N_TILE * n, N_TILE * (n + 1))
+            nc.gpsimd.tensor_scalar(
+                out=normalised[:],
+                in0=scaled[i][:, cols],
+                scalar1=rstd[i][:],
+                scalar2=0.0,
+                op0=ALU.mult,
+                op1=ALU.add,
+            )
             nc.gpsimd.tensor_tensor(
                 out=result[i][:, cols],
-                in0=normalised[:, cols],
-                in1=shift_sb[:].bitcast(BF16)[:, cols],
+                in0=normalised[:],
+                in1=shift_sb[:].bitcast(BF16),
                 op=ALU.add,
             )
 
@@ -244,14 +319,16 @@ def tile_disentangledattention_pc_s_kernel(
                 op1=ALU.add,
             )
 
-        def store(i, cols):
-            nc.sync.dma_start(out=out[i][:, cols], in_=result[i][:, cols])
+        def store(i, cols, engine):
+            engine.dma_start(out=out[i][:, cols], in_=result[i][:, cols])
 
         bias_ps = psum.tile([P, H // PAIR], F32, name="bias_ps")
         gain_ps = psum.tile([P, H // PAIR], F32, name="gain_ps")
         shift_ps = psum.tile([P, H // PAIR], F32, name="shift_ps")
         bias_sb = keep.tile([P, H // PAIR], F32, name="bias_sb")
-        shift_sb = keep.tile([P, H // PAIR], F32, name="shift_sb")
+        gain_sb = keep.tile([P, N_TILE // PAIR], F32, name="gain_sb")
+        shift_sb = keep.tile([P, N_TILE // PAIR], F32, name="shift_sb")
+        half_words = [slice(N_TILE // PAIR * n, N_TILE // PAIR * (n + 1)) for n in range(N_TILES)]
 
         bias_on_psum = bias_ps[:].bitcast(BF16)
         bias_on_sbuf = bias_sb[:].bitcast(BF16)
@@ -259,6 +336,7 @@ def tile_disentangledattention_pc_s_kernel(
 
         ff_t0 = transpose_ff(0, "ff_t")
         group_ff(0, ff_t0)
+        keep_warm(1)
         ff_t1 = transpose_ff(1, "product11")
         group_ff(1, ff_t1)
         keep_warm(1)
@@ -272,6 +350,7 @@ def tile_disentangledattention_pc_s_kernel(
         product0 = [psum.tile([P, N_TILE], F32, name="product0%d" % n) for n in range(N_TILES)]
         multiply(0, product0)
         spread_vector(GAIN, gain_ps)
+        nc.scalar.copy(out=gain_sb[:], in_=gain_ps[:, half_words[1]])
         product1 = [psum.tile([P, N_TILE], F32, name="product1%d" % n) for n in range(N_TILES)]
         multiply(1, product1)
         spread_vector(SHIFT, shift_ps)
@@ -287,19 +366,24 @@ def tile_disentangledattention_pc_s_kernel(
         negative_mean(0)
         add_bias_to_residual(1, slice(384, 512), nc.vector, bias_on_psum)
         deviation(0)
-        nc.scalar.copy(out=shift_sb[:], in_=shift_ps[:])
-        centre_and_gain(0)
-        normalise_on_scalar(0, 1)
-        shift_on_gpsimd(0, 1)
-        store(0, half_cols[1])
+        nc.scalar.copy(out=shift_sb[:], in_=shift_ps[:, half_words[1]])
+        centre_and_gain(0, half_cols[0])
+        centre_and_gain_on_gpsimd(0, 1)
+        normalise_and_shift_on_gpsimd(0, 1)
         add_residual(1, 0, product1)
+        first_half_variance(1)
         add_residual(1, 1, product1)
+        half_squares(1, 1)
         normalise_and_shift(0, slice(0, 256))
         negative_mean(1)
-        deviation(1)
+        mean_offset(1)
         normalise_and_shift(0, slice(256, 512))
-        store(0, half_cols[0])
-        centre_and_gain(1)
+        offset_less_first_half(1)
+        deviation_from_halves(1)
+        store(0, half_cols[1], nc.scalar)
+        store(0, half_cols[0], nc.sync)
+        centre_and_gain(1, half_cols[0])
+        centre_and_gain(1, half_cols[1])
         for n in range(N_TILES):
             normalise_and_shift(1, half_cols[n])
-            store(1, half_cols[n])
+            store(1, half_cols[n], nc.sync)

@@ -50,7 +50,7 @@ def tile_disentangledattention_pc_s_kernel(
                     warm_ps[:], lhsT=warm_src[:], rhs=warm_src[:], start=True, stop=True
                 )
 
-        keep_warm(3)
+        keep_warm(4)
 
         w_scales = keep.tile([P, K_PASSES, H], U8, name="w_scales", align_bytes=64)
         nc.vector.memset(w_scales[:].bitcast(I32), 0)
@@ -61,7 +61,10 @@ def tile_disentangledattention_pc_s_kernel(
 
         ff_sb = [keep.tile([P, K], BF16, name="ff_sb%d" % i) for i in range(TOKEN_TILES)]
         attn_sb = [keep.tile([P, H], BF16, name="attn_sb%d" % i) for i in range(TOKEN_TILES)]
-        w_words = keep.tile([P, K_PASSES, 2 * H], U8, name="w_words", align_bytes=64)
+        w_words = [
+            keep.tile([P, K_PASSES, 2 * N_TILE], U8, name="w_words%d" % n, align_bytes=64)
+            for n in range(N_TILES)
+        ]
 
         vector_words = keep.tile([P, 3, 2 * VECTOR_WORDS * PAIR], BF16, name="vector_words")
 
@@ -71,13 +74,19 @@ def tile_disentangledattention_pc_s_kernel(
                 in_=vector.rearrange("(p w) -> p w", w=VECTOR_WORDS * PAIR),
             )
 
+        def load_weights(n):
+            cols = slice(2 * N_TILE * n, 2 * N_TILE * (n + 1))
+            nc.sync.dma_start(
+                out=w_words[n][:].bitcast(I32),
+                in_=Wf_words.rearrange("g p n -> p g n")[:, :, cols].bitcast(I32),
+            )
+
         nc.sync.dma_start(out=ff_sb[0][:], in_=ff[0])
         load_vector(BIAS, b_f)
+        table_warmer = keep.tile([P, 1], F32, name="table_warmer")
+        nc.scalar.activation(out=table_warmer[:], in_=eps[:], func=ACT.Abs_reciprocal_sqrt)
         nc.sync.dma_start(out=ff_sb[1][:], in_=ff[1])
-        load_vector(GAIN, ln2_g)
-        nc.sync.dma_start(
-            out=w_words[:].bitcast(I32), in_=Wf_words.rearrange("g p n -> p g n").bitcast(I32)
-        )
+        load_weights(0)
         for quadrant in range(4):
             nc.sync.dma_start(
                 out=w_scales[32 * quadrant : 32 * quadrant + 4].bitcast(I32),
@@ -86,10 +95,8 @@ def tile_disentangledattention_pc_s_kernel(
                 .bitcast(I32),
             )
         nc.sync.dma_start(out=attn_sb[0][:], in_=attn_out[0])
+        load_weights(1)
         nc.sync.dma_start(out=attn_sb[1][:], in_=attn_out[1])
-        table_warmer = keep.tile([P, 1], F32, name="table_warmer")
-        nc.scalar.activation(out=table_warmer[:], in_=eps[:], func=ACT.Abs_reciprocal_sqrt)
-        load_vector(SHIFT, ln2_b)
 
         def spread_vector(v, spread_ps):
             words = vector_words[:, v, 0 : VECTOR_WORDS * PAIR].bitcast(F32)
@@ -113,22 +120,19 @@ def tile_disentangledattention_pc_s_kernel(
             for i in range(TOKEN_TILES)
         ]
 
-        def transpose_ff(i, bank_tag):
-            ff_t = psum.tile([P, K_PASSES, PAIR, P], F32, name="ff_t%d" % i, tag=bank_tag)
+        def transpose_ff(i, g, bank_tag):
+            ff_t = psum.tile([P, PAIR, P], F32, name="ff_t%d%d" % (i, g), tag=bank_tag)
             words = ff_sb[i][:].bitcast(F32)
-            for g in range(K_PASSES):
-                for u in range(PAIR):
-                    nc.tensor.transpose(
-                        ff_t[:, g, u, :],
-                        words[:, WORDS_PER_PASS * g + u : WORDS_PER_PASS * (g + 1) : PAIR],
-                        identity[:],
-                    )
+            for u in range(PAIR):
+                nc.tensor.transpose(
+                    ff_t[:, u, :],
+                    words[:, WORDS_PER_PASS * g + u : WORDS_PER_PASS * (g + 1) : PAIR],
+                    identity[:],
+                )
             return ff_t
 
-        def group_ff(i, ff_t):
-            nc.scalar.copy(
-                out=ff_grouped[i][:].bitcast(F32), in_=ff_t[:].rearrange("p g u r -> p g r u")
-            )
+        def group_ff(i, g, ff_t, copy):
+            copy(out=ff_grouped[i][:, g].bitcast(F32), in_=ff_t[:].rearrange("p u r -> p r u"))
 
         def quantise_ff(i):
             nc.vector.quantize_mx(
@@ -144,7 +148,7 @@ def tile_disentangledattention_pc_s_kernel(
                         out=product[n][:],
                         lhsT=ff_codes[i][:, g * P : (g + 1) * P].bitcast(FP8X4),
                         lhsT_scale=ff_scales[i][:, g * P : (g + 1) * P],
-                        rhs=w_words[:, g, 2 * N_TILE * n : 2 * N_TILE * (n + 1)].bitcast(FP4X4),
+                        rhs=w_words[n][:, g, :].bitcast(FP4X4),
                         rhs_scale=w_scales[:, g, N_TILE * n : N_TILE * (n + 1)],
                         start=(g == 0),
                         stop=(g == K_PASSES - 1),
@@ -164,11 +168,20 @@ def tile_disentangledattention_pc_s_kernel(
         neg_rest = keep.tile([P, 1], F32, name="neg_rest")
         rstd = [keep.tile([P, 1], F32, name="rstd%d" % i) for i in range(TOKEN_TILES)]
 
-        def add_bias_to_residual(i, cols, engine, bias_bf16):
-            engine.tensor_tensor(
+        def add_bias_to_residual(i, cols):
+            nc.vector.tensor_tensor(
                 out=residual[i][:, cols],
                 in0=attn_sb[i][:, cols],
-                in1=bias_bf16[:, cols],
+                in1=bias_ps[:].bitcast(BF16)[:, cols],
+                op=ALU.add,
+            )
+
+        def add_bias_to_residual_on_gpsimd(i, n):
+            cols = slice(N_TILE * n, N_TILE * (n + 1))
+            nc.gpsimd.tensor_tensor(
+                out=residual[i][:, cols],
+                in0=attn_sb[i][:, cols],
+                in1=bias_sb[:].bitcast(BF16),
                 op=ALU.add,
             )
 
@@ -325,25 +338,28 @@ def tile_disentangledattention_pc_s_kernel(
         bias_ps = psum.tile([P, H // PAIR], F32, name="bias_ps")
         gain_ps = psum.tile([P, H // PAIR], F32, name="gain_ps")
         shift_ps = psum.tile([P, H // PAIR], F32, name="shift_ps")
-        bias_sb = keep.tile([P, H // PAIR], F32, name="bias_sb")
+        bias_sb = keep.tile([P, N_TILE // PAIR], F32, name="bias_sb")
         gain_sb = keep.tile([P, N_TILE // PAIR], F32, name="gain_sb")
         shift_sb = keep.tile([P, N_TILE // PAIR], F32, name="shift_sb")
         half_words = [slice(N_TILE // PAIR * n, N_TILE // PAIR * (n + 1)) for n in range(N_TILES)]
 
-        bias_on_psum = bias_ps[:].bitcast(BF16)
-        bias_on_sbuf = bias_sb[:].bitcast(BF16)
         half_cols = [slice(N_TILE * n, N_TILE * (n + 1)) for n in range(N_TILES)]
 
-        ff_t0 = transpose_ff(0, "ff_t")
-        group_ff(0, ff_t0)
+        ff_t00 = transpose_ff(0, 0, "ff_t")
+        group_ff(0, 0, ff_t00, nc.scalar.copy)
+        ff_t01 = transpose_ff(0, 1, "product11")
+        group_ff(0, 1, ff_t01, nc.vector.tensor_copy)
+        quantise_ff(0)
         keep_warm(1)
-        ff_t1 = transpose_ff(1, "product11")
-        group_ff(1, ff_t1)
-        keep_warm(1)
+        ff_t10 = transpose_ff(1, 0, "product00")
+        group_ff(1, 0, ff_t10, nc.scalar.copy)
+        ff_t11 = transpose_ff(1, 1, "product01")
+        group_ff(1, 1, ff_t11, nc.vector.tensor_copy)
         spread_vector(BIAS, bias_ps)
         keep_warm(2)
-        nc.scalar.copy(out=bias_sb[:], in_=bias_ps[:])
-        quantise_ff(0)
+        nc.scalar.copy(out=bias_sb[:], in_=bias_ps[:, half_words[1]])
+        load_vector(GAIN, ln2_g)
+        load_vector(SHIFT, ln2_b)
         keep_warm(1)
         quantise_ff(1)
 
@@ -355,16 +371,16 @@ def tile_disentangledattention_pc_s_kernel(
         multiply(1, product1)
         spread_vector(SHIFT, shift_ps)
 
-        add_bias_to_residual(0, half_cols[0], nc.vector, bias_on_psum)
-        add_bias_to_residual(0, half_cols[1], nc.gpsimd, bias_on_sbuf)
-        add_bias_to_residual(1, half_cols[1], nc.gpsimd, bias_on_sbuf)
+        add_bias_to_residual(0, half_cols[0])
+        add_bias_to_residual_on_gpsimd(0, 1)
+        add_bias_to_residual_on_gpsimd(1, 1)
 
         add_residual(0, 0, product0)
-        add_bias_to_residual(1, slice(0, 256), nc.vector, bias_on_psum)
+        add_bias_to_residual(1, slice(0, 256))
         add_residual(0, 1, product0)
-        add_bias_to_residual(1, slice(256, 384), nc.vector, bias_on_psum)
+        add_bias_to_residual(1, slice(256, 384))
         negative_mean(0)
-        add_bias_to_residual(1, slice(384, 512), nc.vector, bias_on_psum)
+        add_bias_to_residual(1, slice(384, 512))
         deviation(0)
         nc.scalar.copy(out=shift_sb[:], in_=shift_ps[:, half_words[1]])
         centre_and_gain(0, half_cols[0])

@@ -306,21 +306,22 @@ def tile_disentangledattention_pc_s_kernel(
         normalised = keep.tile([P, N_TILE], F32, name="normalised")
 
         def normalise_and_shift_on_gpsimd(i, n):
-            cols = slice(N_TILE * n, N_TILE * (n + 1))
-            nc.gpsimd.tensor_scalar(
-                out=normalised[:],
-                in0=scaled[i][:, cols],
-                scalar1=rstd[i][:],
-                scalar2=0.0,
-                op0=ALU.mult,
-                op1=ALU.add,
-            )
-            nc.gpsimd.tensor_tensor(
-                out=result[i][:, cols],
-                in0=normalised[:],
-                in1=shift_sb[:].bitcast(BF16),
-                op=ALU.add,
-            )
+            for quarter in (slice(0, N_TILE // 2), slice(N_TILE // 2, N_TILE)):
+                cols = slice(N_TILE * n + quarter.start, N_TILE * n + quarter.stop)
+                nc.gpsimd.tensor_scalar(
+                    out=normalised[:, quarter],
+                    in0=scaled[i][:, cols],
+                    scalar1=rstd[i][:],
+                    scalar2=0.0,
+                    op0=ALU.mult,
+                    op1=ALU.add,
+                )
+                nc.gpsimd.tensor_tensor(
+                    out=result[i][:, cols],
+                    in0=normalised[:, quarter],
+                    in1=shift_sb[:].bitcast(BF16)[:, quarter],
+                    op=ALU.add,
+                )
 
         def normalise_and_shift(i, cols):
             nc.vector.scalar_tensor_tensor(
@@ -346,15 +347,15 @@ def tile_disentangledattention_pc_s_kernel(
         half_cols = [slice(N_TILE * n, N_TILE * (n + 1)) for n in range(N_TILES)]
 
         ff_t00 = transpose_ff(0, 0, "ff_t")
-        group_ff(0, 0, ff_t00, nc.scalar.copy)
+        group_ff(0, 0, ff_t00, nc.vector.tensor_copy)
         ff_t01 = transpose_ff(0, 1, "product11")
-        group_ff(0, 1, ff_t01, nc.vector.tensor_copy)
+        group_ff(0, 1, ff_t01, nc.scalar.copy)
         quantise_ff(0)
         keep_warm(1)
         ff_t10 = transpose_ff(1, 0, "product00")
-        group_ff(1, 0, ff_t10, nc.scalar.copy)
+        group_ff(1, 0, ff_t10, nc.vector.tensor_copy)
         ff_t11 = transpose_ff(1, 1, "product01")
-        group_ff(1, 1, ff_t11, nc.vector.tensor_copy)
+        group_ff(1, 1, ff_t11, nc.scalar.copy)
         spread_vector(BIAS, bias_ps)
         keep_warm(2)
         nc.scalar.copy(out=bias_sb[:], in_=bias_ps[:, half_words[1]])
@@ -376,11 +377,10 @@ def tile_disentangledattention_pc_s_kernel(
         add_bias_to_residual_on_gpsimd(1, 1)
 
         add_residual(0, 0, product0)
-        add_bias_to_residual(1, slice(0, 256))
         add_residual(0, 1, product0)
-        add_bias_to_residual(1, slice(256, 384))
+        add_bias_to_residual(1, slice(0, 256))
         negative_mean(0)
-        add_bias_to_residual(1, slice(384, 512))
+        add_bias_to_residual(1, slice(256, 512))
         deviation(0)
         nc.scalar.copy(out=shift_sb[:], in_=shift_ps[:, half_words[1]])
         centre_and_gain(0, half_cols[0])
@@ -396,10 +396,16 @@ def tile_disentangledattention_pc_s_kernel(
         normalise_and_shift(0, slice(256, 512))
         offset_less_first_half(1)
         deviation_from_halves(1)
-        store(0, half_cols[1], nc.scalar)
+        for quarter in (slice(512, 768), slice(768, 1024)):
+            store(0, quarter, nc.scalar)
         store(0, half_cols[0], nc.sync)
+        third_quarter, last_quarter = slice(512, 768), slice(768, 1024)
         centre_and_gain(1, half_cols[0])
-        centre_and_gain(1, half_cols[1])
-        for n in range(N_TILES):
-            normalise_and_shift(1, half_cols[n])
-            store(1, half_cols[n], nc.sync)
+        centre_and_gain(1, third_quarter)
+        normalise_and_shift(1, half_cols[0])
+        store(1, half_cols[0], nc.sync)
+        centre_and_gain(1, last_quarter)
+        normalise_and_shift(1, third_quarter)
+        store(1, third_quarter, nc.sync)
+        normalise_and_shift(1, last_quarter)
+        store(1, last_quarter, nc.sync)

from contextlib import ExitStack

import concourse.mybir as mybir
from concourse.masks import make_identity

F32 = mybir.dt.float32
BF16 = mybir.dt.bfloat16
I32 = mybir.dt.int32
U32 = mybir.dt.uint32
U8 = mybir.dt.uint8
FP8X4 = mybir.dt.float8_e4m3fn_x4
FP4X4 = mybir.dt.float4_e2m1fn_x4
ALU = mybir.AluOpType
ACT = mybir.ActivationFunctionType

P = 128
PACK = 4
K_PASS = P * PACK
TOKEN_TILES = 2
K = 1024
H = 1024
K_PASSES = K // K_PASS
N_TILE = 512
N_TILES = H // N_TILE
PAIR = 2
WORDS_PER_PASS = K_PASS // PAIR
VECTOR_WORDS = H // (PAIR * P)
EPS = 1e-7
BIAS, GAIN, SHIFT = 0, 1, 2

FLOPS = 2 * TOKEN_TILES * P * K * H


def tile_disentangledattention_pc_s_kernel(
    tc, ff, attn_out, Wf_words, Wf_scales, b_f, ln2_g, ln2_b, out
):
    nc = tc.nc
    with ExitStack() as ctx:
        keep = ctx.enter_context(tc.tile_pool(name="keep", bufs=1))
        psum = ctx.enter_context(tc.psum_pool(name="psum", bufs=1))
        ctx.enter_context(tc.manual_schedule())

        warm_src = keep.tile([P, P], F32, name="warm_src")
        nc.gpsimd.memset(warm_src[:], 0.0)
        warm_ps = psum.tile([P, P], F32, name="warm_ps", tag="product10")

        def keep_warm(count):
            for unused in range(count):
                nc.tensor.matmul(
                    warm_ps[:], lhsT=warm_src[:], rhs=warm_src[:], start=True, stop=True
                )

        keep_warm(4)

        w_scales = keep.tile([P, K_PASSES, H], U8, name="w_scales", align_bytes=64)
        nc.vector.memset(w_scales[:].bitcast(I32), 0)
        eps = keep.tile([P, 1], F32, name="eps")
        nc.vector.memset(eps[:], EPS)
        identity = keep.tile([P, P], F32, name="identity")
        make_identity(nc, identity[:])

        ff_sb = [keep.tile([P, K], BF16, name="ff_sb%d" % i) for i in range(TOKEN_TILES)]
        attn_sb = [keep.tile([P, H], BF16, name="attn_sb%d" % i) for i in range(TOKEN_TILES)]
        w_words = [
            keep.tile([P, K_PASSES, 2 * N_TILE], U8, name="w_words%d" % n, align_bytes=64)
            for n in range(N_TILES)
        ]

        vector_words = keep.tile([P, 3, 2 * VECTOR_WORDS * PAIR], BF16, name="vector_words")

        def load_vector(v, vector):
            nc.scalar.dma_start(
                out=vector_words[:, v, 0 : VECTOR_WORDS * PAIR],
                in_=vector.rearrange("(p w) -> p w", w=VECTOR_WORDS * PAIR),
            )

        def load_weights(n):
            cols = slice(2 * N_TILE * n, 2 * N_TILE * (n + 1))
            nc.sync.dma_start(
                out=w_words[n][:].bitcast(I32),
                in_=Wf_words.rearrange("g p n -> p g n")[:, :, cols].bitcast(I32),
            )

        nc.sync.dma_start(out=ff_sb[0][:], in_=ff[0])
        load_vector(BIAS, b_f)
        table_warmer = keep.tile([P, 1], F32, name="table_warmer")
        nc.scalar.activation(out=table_warmer[:], in_=eps[:], func=ACT.Abs_reciprocal_sqrt)
        nc.sync.dma_start(out=ff_sb[1][:], in_=ff[1])
        load_weights(0)
        for quadrant in range(4):
            nc.sync.dma_start(
                out=w_scales[32 * quadrant : 32 * quadrant + 4].bitcast(I32),
                in_=Wf_scales[:, 4 * quadrant : 4 * quadrant + 4, :]
                .rearrange("g r n -> r g n")
                .bitcast(I32),
            )
        nc.sync.dma_start(out=attn_sb[0][:], in_=attn_out[0])
        load_weights(1)
        nc.sync.dma_start(out=attn_sb[1][:], in_=attn_out[1])

        def spread_vector(v, spread_ps):
            words = vector_words[:, v, 0 : VECTOR_WORDS * PAIR].bitcast(F32)
            for c in range(VECTOR_WORDS):
                nc.tensor.transpose(
                    spread_ps[:, c : H // PAIR : VECTOR_WORDS],
                    words[:, c : c + 1].to_broadcast([P, P]),
                    identity[:],
                )

        ff_codes = [
            keep.tile([P, K_PASSES * P], U32, name="ff_codes%d" % i, align_bytes=64)
            for i in range(TOKEN_TILES)
        ]
        ff_scales = [
            keep.tile([P, K_PASSES * P], U8, name="ff_scales%d" % i, align_bytes=64)
            for i in range(TOKEN_TILES)
        ]
        ff_grouped = [
            keep.tile([P, K_PASSES, P, PACK], BF16, name="ff_grouped%d" % i, align_bytes=64)
            for i in range(TOKEN_TILES)
        ]

        def transpose_ff(i, g, bank_tag):
            ff_t = psum.tile([P, PAIR, P], F32, name="ff_t%d%d" % (i, g), tag=bank_tag)
            words = ff_sb[i][:].bitcast(F32)
            for u in range(PAIR):
                nc.tensor.transpose(
                    ff_t[:, u, :],
                    words[:, WORDS_PER_PASS * g + u : WORDS_PER_PASS * (g + 1) : PAIR],
                    identity[:],
                )
            return ff_t

        def group_ff(i, g, ff_t, copy):
            copy(out=ff_grouped[i][:, g].bitcast(F32), in_=ff_t[:].rearrange("p u r -> p r u"))

        def quantise_ff(i):
            nc.vector.quantize_mx(
                out=ff_codes[i][:].bitcast(FP8X4),
                scales=ff_scales[i][:],
                in_=ff_grouped[i][:].rearrange("p g r t -> p (g r t)"),
            )

        def multiply(i, product):
            for n in range(N_TILES):
                for g in range(K_PASSES):
                    nc.tensor.matmul_mx(
                        out=product[n][:],
                        lhsT=ff_codes[i][:, g * P : (g + 1) * P].bitcast(FP8X4),
                        lhsT_scale=ff_scales[i][:, g * P : (g + 1) * P],
                        rhs=w_words[n][:, g, :].bitcast(FP4X4),
                        rhs_scale=w_scales[:, g, N_TILE * n : N_TILE * (n + 1)],
                        start=(g == 0),
                        stop=(g == K_PASSES - 1),
                    )

        residual = [keep.tile([P, H], F32, name="residual%d" % i) for i in range(TOKEN_TILES)]
        u = [keep.tile([P, H], F32, name="u%d" % i) for i in range(TOKEN_TILES)]
        squares = [keep.tile([P, H], BF16, name="squares%d" % i) for i in range(TOKEN_TILES)]
        scaled = [keep.tile([P, H], F32, name="scaled%d" % i) for i in range(TOKEN_TILES)]
        result = [keep.tile([P, H], F32, name="result%d" % i) for i in range(TOKEN_TILES)]
        sums = [keep.tile([P, N_TILES], F32, name="sums%d" % i) for i in range(TOKEN_TILES)]
        neg_mean = [keep.tile([P, 1], F32, name="neg_mean%d" % i) for i in range(TOKEN_TILES)]
        sum_sq = [keep.tile([P, 1], F32, name="sum_sq%d" % i) for i in range(TOKEN_TILES)]
        half_sq = keep.tile([P, N_TILES], F32, name="half_sq")
        first_var = keep.tile([P, 1], F32, name="first_var")
        offset = keep.tile([P, 1], F32, name="offset")
        neg_rest = keep.tile([P, 1], F32, name="neg_rest")
        rstd = [keep.tile([P, 1], F32, name="rstd%d" % i) for i in range(TOKEN_TILES)]

        def add_bias_to_residual(i, cols):
            nc.vector.tensor_tensor(
                out=residual[i][:, cols],
                in0=attn_sb[i][:, cols],
                in1=bias_ps[:].bitcast(BF16)[:, cols],
                op=ALU.add,
            )

        def add_bias_to_residual_on_gpsimd(i, n):
            cols = slice(N_TILE * n, N_TILE * (n + 1))
            nc.gpsimd.tensor_tensor(
                out=residual[i][:, cols],
                in0=attn_sb[i][:, cols],
                in1=bias_sb[:].bitcast(BF16),
                op=ALU.add,
            )

        def add_residual(i, n, product):
            cols = slice(N_TILE * n, N_TILE * (n + 1))
            nc.vector.scalar_tensor_tensor(
                out=u[i][:, cols],
                in0=product[n][:],
                scalar=1.0,
                in1=residual[i][:, cols],
                op0=ALU.mult,
                op1=ALU.add,
                accum_out=sums[i][:, n : n + 1],
            )

        def negative_mean(i):
            nc.vector.tensor_scalar(
                out=neg_mean[i][:],
                in0=sums[i][:, 0:1],
                scalar1=sums[i][:, 1:2],
                scalar2=-1.0 / H,
                op0=ALU.add,
                op1=ALU.mult,
            )

        def deviation(i):
            nc.scalar.activation(
                out=squares[i][:],
                in_=u[i][:],
                func=ACT.Square,
                bias=neg_mean[i][:],
                scale=1.0,
                accum_out=sum_sq[i][:],
            )
            nc.scalar.activation(
                out=rstd[i][:],
                in_=sum_sq[i][:],
                func=ACT.Abs_reciprocal_sqrt,
                bias=eps[:],
                scale=1.0 / H,
            )

        def half_squares(i, n):
            cols = slice(N_TILE * n, N_TILE * (n + 1))
            nc.scalar.activation(
                out=squares[i][:, cols],
                in_=u[i][:, cols],
                func=ACT.Square,
                bias=sums[i][:, 0:1],
                scale=-float(N_TILE),
                accum_out=half_sq[:, n : n + 1],
            )

        def first_half_variance(i):
            half_squares(i, 0)
            nc.scalar.activation(
                out=first_var[:],
                in_=half_sq[:, 0:1],
                func=ACT.Identity,
                bias=eps[:],
                scale=1.0 / (H * N_TILE * N_TILE),
            )

        def mean_offset(i):
            nc.vector.tensor_scalar(
                out=offset[:],
                in0=sums[i][:, 1:2],
                scalar1=sums[i][:, 0:1],
                scalar2=1.0 / H,
                op0=ALU.subtract,
                op1=ALU.mult,
            )

        def offset_less_first_half(i):
            nc.vector.tensor_scalar(
                out=neg_rest[:],
                in0=offset[:],
                scalar1=offset[:],
                scalar2=first_var[:],
                op0=ALU.mult,
                op1=ALU.subtract,
            )

        def deviation_from_halves(i):
            nc.scalar.activation(
                out=rstd[i][:],
                in_=half_sq[:, 1:2],
                func=ACT.Abs_reciprocal_sqrt,
                bias=neg_rest[:],
                scale=-1.0 / (H * N_TILE * N_TILE),
            )

        def centre_and_gain(i, cols):
            nc.vector.scalar_tensor_tensor(
                out=scaled[i][:, cols],
                in0=u[i][:, cols],
                scalar=neg_mean[i][:],
                in1=gain_ps[:].bitcast(BF16)[:, cols],
                op0=ALU.add,
                op1=ALU.mult,
            )

        centred = keep.tile([P, N_TILE], F32, name="centred")

        def centre_and_gain_on_gpsimd(i, n):
            cols = slice(N_TILE * n, N_TILE * (n + 1))
            nc.gpsimd.tensor_scalar(
                out=centred[:],
                in0=u[i][:, cols],
                scalar1=neg_mean[i][:],
                scalar2=1.0,
                op0=ALU.add,
                op1=ALU.mult,
            )
            nc.gpsimd.tensor_tensor(
                out=scaled[i][:, cols],
                in0=centred[:],
                in1=gain_sb[:].bitcast(BF16),
                op=ALU.mult,
            )

        normalised = keep.tile([P, N_TILE], F32, name="normalised")

        def normalise_and_shift_on_gpsimd(i, n):
            for quarter in (slice(0, N_TILE // 2), slice(N_TILE // 2, N_TILE)):
                cols = slice(N_TILE * n + quarter.start, N_TILE * n + quarter.stop)
                nc.gpsimd.tensor_scalar(
                    out=normalised[:, quarter],
                    in0=scaled[i][:, cols],
                    scalar1=rstd[i][:],
                    scalar2=0.0,
                    op0=ALU.mult,
                    op1=ALU.add,
                )
                nc.gpsimd.tensor_tensor(
                    out=result[i][:, cols],
                    in0=normalised[:, quarter],
                    in1=shift_sb[:].bitcast(BF16)[:, quarter],
                    op=ALU.add,
                )

        def normalise_and_shift(i, cols):
            nc.vector.scalar_tensor_tensor(
                out=result[i][:, cols],
                in0=scaled[i][:, cols],
                scalar=rstd[i][:],
                in1=shift_ps[:].bitcast(BF16)[:, cols],
                op0=ALU.mult,
                op1=ALU.add,
            )

        def store(i, cols, engine):
            engine.dma_start(out=out[i][:, cols], in_=result[i][:, cols])

        bias_ps = psum.tile([P, H // PAIR], F32, name="bias_ps")
        gain_ps = psum.tile([P, H // PAIR], F32, name="gain_ps")
        shift_ps = psum.tile([P, H // PAIR], F32, name="shift_ps")
        bias_sb = keep.tile([P, N_TILE // PAIR], F32, name="bias_sb")
        gain_sb = keep.tile([P, N_TILE // PAIR], F32, name="gain_sb")
        shift_sb = keep.tile([P, N_TILE // PAIR], F32, name="shift_sb")
        half_words = [slice(N_TILE // PAIR * n, N_TILE // PAIR * (n + 1)) for n in range(N_TILES)]

        half_cols = [slice(N_TILE * n, N_TILE * (n + 1)) for n in range(N_TILES)]

        ff_t00 = transpose_ff(0, 0, "ff_t")
        group_ff(0, 0, ff_t00, nc.vector.tensor_copy)
        ff_t01 = transpose_ff(0, 1, "product11")
        group_ff(0, 1, ff_t01, nc.scalar.copy)
        quantise_ff(0)
        keep_warm(1)
        ff_t10 = transpose_ff(1, 0, "product00")
        group_ff(1, 0, ff_t10, nc.vector.tensor_copy)
        ff_t11 = transpose_ff(1, 1, "product01")
        group_ff(1, 1, ff_t11, nc.scalar.copy)
        spread_vector(BIAS, bias_ps)
        keep_warm(2)
        nc.scalar.copy(out=bias_sb[:], in_=bias_ps[:, half_words[1]])
        load_vector(GAIN, ln2_g)
        load_vector(SHIFT, ln2_b)
        keep_warm(1)
        quantise_ff(1)

        product0 = [psum.tile([P, N_TILE], F32, name="product0%d" % n) for n in range(N_TILES)]
        multiply(0, product0)
        spread_vector(GAIN, gain_ps)
        nc.scalar.copy(out=gain_sb[:], in_=gain_ps[:, half_words[1]])
        product1 = [psum.tile([P, N_TILE], F32, name="product1%d" % n) for n in range(N_TILES)]
        multiply(1, product1)
        spread_vector(SHIFT, shift_ps)

        add_bias_to_residual(0, half_cols[0])
        add_bias_to_residual_on_gpsimd(0, 1)
        add_bias_to_residual_on_gpsimd(1, 1)

        add_residual(0, 0, product0)
        add_residual(0, 1, product0)
        add_bias_to_residual(1, slice(0, 256))
        negative_mean(0)
        add_bias_to_residual(1, slice(256, 512))
        deviation(0)
        nc.scalar.copy(out=shift_sb[:], in_=shift_ps[:, half_words[1]])
        centre_and_gain(0, half_cols[0])
        centre_and_gain_on_gpsimd(0, 1)
        normalise_and_shift_on_gpsimd(0, 1)
        add_residual(1, 0, product1)
        first_half_variance(1)
        add_residual(1, 1, product1)
        half_squares(1, 1)
        normalise_and_shift(0, slice(0, 256))
        negative_mean(1)
        mean_offset(1)
        normalise_and_shift(0, slice(256, 512))
        offset_less_first_half(1)
        deviation_from_halves(1)
        for quarter in (slice(512, 768), slice(768, 1024)):
            store(0, quarter, nc.scalar)
        store(0, half_cols[0], nc.sync)
        third_quarter, last_quarter = slice(512, 768), slice(768, 1024)
        centre_and_gain(1, half_cols[0])
        centre_and_gain(1, third_quarter)
        normalise_and_shift(1, half_cols[0])
        store(1, half_cols[0], nc.sync)
        centre_and_gain(1, last_quarter)
        normalise_and_shift(1, third_quarter)
        store(1, third_quarter, nc.sync)
        normalise_and_shift(1, last_quarter)
        store(1, last_quarter, nc.sync)
